import numpy as np
import ml_dtypes


def mxq(x, axis, fmt="e4m3"):
    dtype, down = {"e4m3": (ml_dtypes.float8_e4m3fn, 7), "e5m2": (ml_dtypes.float8_e5m2, 14)}[fmt]
    v = np.moveaxis(np.asarray(x, np.float32).astype(ml_dtypes.bfloat16).astype(np.float64), axis, -1)
    blocks = v.reshape(v.shape[:-1] + (-1, 32))
    amax = np.abs(blocks).max(-1, keepdims=True)
    byte = np.maximum(np.where(amax > 0, np.frexp(amax)[1] - 1 + 127, 0) - down, 1)
    scale = np.exp2(byte - 127.0)
    codes = (blocks / scale).astype(np.float32).astype(dtype).astype(np.float64)
    return np.moveaxis((codes * scale).reshape(v.shape), -1, axis)


WIDE = False


def mx_kscale(k):
    if not WIDE:
        return np.ones(k)
    levels = np.array([10, -10, 5, -5, 0])
    a = np.random.permutation(np.resize(levels, k // 512 * 4)).reshape(k // 512, 4)
    idx = np.arange(k)
    return np.exp2(a[idx // 512, idx % 128 // 32])


BF16 = ml_dtypes.bfloat16


def bf(x):
    return np.asarray(x, np.float32).astype(BF16)


def f64(x):
    return np.asarray(x).astype(np.float64)


B, S, D_IN, D_H = 4096, 256, 256, 512
H_IN = 2 * S + D_IN


def setup_inputs():
    t = mx_kscale(D_H)
    return {"h1": bf(np.tanh(np.random.standard_normal((B, D_H)) * 0.8)),
            "u": bf(np.random.standard_normal((B, D_H)) * t),
            "W1_qp": bf(np.random.standard_normal((2 * S, D_H)) * 0.8 / np.sqrt(H_IN) / t[None, :]),
            "q": bf(np.random.standard_normal((B, S))),
            "p": bf(np.random.standard_normal((B, S))),
            "dt": bf(0.3 + 0.2 * np.random.random(1)),
            "W_out": bf(np.random.standard_normal((2 * S, D_IN)) / np.sqrt(2 * S)),
            "b_out": bf(np.random.standard_normal(D_IN) * 0.3)}


def reference(h1, u, W1_qp, q, p, dt, W_out, b_out):
    h1, q, p, dt = f64(h1), f64(q), f64(p), f64(dt)
    g1 = (1.0 - h1 * h1) * f64(u)
    g_qp = mxq(g1, 1, "e4m3") @ mxq(f64(W1_qp), 1, "e4m3").T
    dH_dq = g_qp[:, :S]
    dH_dp = g_qp[:, S:]
    q_new = q + dt * dH_dp
    p_new = p + dt * (-dH_dq)
    state = np.concatenate([q_new, p_new], axis=-1)
    output = (mxq(state, 1, "e4m3") @ mxq(f64(W_out), 0, "e4m3")) + f64(b_out)
    return output, q_new, p_new

@@ -1,0 +1,258 @@
+from contextlib import ExitStack
+
+import concourse.mybir as mybir
+from concourse.masks import make_identity
+
+BF16 = mybir.dt.bfloat16
+F32 = mybir.dt.float32
+U32 = mybir.dt.uint32
+U8 = mybir.dt.uint8
+FP8X4 = mybir.dt.float8_e4m3fn_x4
+ALU = mybir.AluOpType
+ACT = mybir.ActivationFunctionType
+
+P = 128
+PACK = 4
+BATCH = 4096
+HALF = 256
+K = 512
+TILES = BATCH // P
+PAIR = 2
+PAIRS = TILES // PAIR
+COLS = PAIR * P
+CHUNK = 4
+CHUNKS = TILES // CHUNK
+PSUM_BANKS = 8
+
+FLOPS = 2 * BATCH * K * K + 2 * BATCH * K * HALF
+
+
+def tile_timecrystalblock_pb_t_kernel(
+    tc, h1, u, W1_qp, q, p, dt, W_out, b_out, out_0, out_1, out_2
+):
+    nc = tc.nc
+
+    h1_rows = h1.rearrange("(p s) k -> p s k", s=TILES)
+    u_rows = u.rearrange("(p s) k -> p s k", s=TILES)
+    q_rows = q.rearrange("(p s) c -> p s c", s=TILES)
+    p_rows = p.rearrange("(p s) c -> p s c", s=TILES)
+    output_rows = out_0.rearrange("(p s) c -> p s c", s=TILES)
+    q_new_rows = out_1.rearrange("(p s) c -> p s c", s=TILES)
+    p_new_rows = out_2.rearrange("(p s) c -> p s c", s=TILES)
+
+    with ExitStack() as ctx:
+        const = ctx.enter_context(tc.tile_pool(name="const", bufs=1))
+        inputs = ctx.enter_context(tc.tile_pool(name="inputs", bufs=CHUNKS))
+        results = ctx.enter_context(tc.tile_pool(name="results", bufs=4))
+        work = ctx.enter_context(tc.tile_pool(name="work", bufs=2))
+        banks = ctx.enter_context(tc.psum_pool(name="banks", bufs=PSUM_BANKS))
+        ctx.enter_context(tc.manual_schedule())
+
+        ident_bf16 = const.tile([P, P], BF16)
+        make_identity(nc, ident_bf16[:])
+        ident_f32 = const.tile([P, P], F32)
+        make_identity(nc, ident_f32[:])
+        ones = const.tile([P, P], BF16)
+        nc.vector.memset(ones[:], 1.0)
+        small_row = const.tile([P, K], BF16)
+        nc.vector.memset(small_row[:], 0.0)
+
+        nc.sync.dma_start(out=small_row[0:1, 0:HALF], in_=b_out.unsqueeze(0))
+        nc.sync.dma_start(out=small_row[0:1, HALF : HALF + 1], in_=dt.unsqueeze(0))
+        w1_sb = const.tile([P, PACK, K], BF16)
+        nc.sync.dma_start(out=w1_sb[:], in_=W1_qp.rearrange("(a p) k -> p a k", p=P))
+        wout_sb = const.tile([P, PACK, HALF], BF16)
+        nc.sync.dma_start(out=wout_sb[:], in_=W_out.rearrange("(t p) c -> p t c", p=P))
+        h1_chunks, u_chunks, q_chunks, p_chunks = [], [], [], []
+        for c in range(CHUNKS):
+            tiles = slice(c * CHUNK, (c + 1) * CHUNK)
+            h1_sb = inputs.tile([P, CHUNK, K], BF16)
+            nc.sync.dma_start(out=h1_sb[:], in_=h1_rows[:, tiles, :])
+            u_sb = inputs.tile([P, CHUNK, K], BF16)
+            nc.sync.dma_start(out=u_sb[:], in_=u_rows[:, tiles, :])
+            q_sb = inputs.tile([P, CHUNK, HALF], BF16)
+            nc.sync.dma_start(out=q_sb[:], in_=q_rows[:, tiles, :])
+            p_sb = inputs.tile([P, CHUNK, HALF], BF16)
+            nc.sync.dma_start(out=p_sb[:], in_=p_rows[:, tiles, :])
+            h1_chunks.append(h1_sb)
+            u_chunks.append(u_sb)
+            q_chunks.append(q_sb)
+            p_chunks.append(p_sb)
+
+        def transpose_pair(rows_sb, first):
+            planes = banks.tile([P, PACK, COLS], BF16, tag="bank")
+            for i in range(PAIR):
+                for t in range(PACK):
+                    nc.tensor.transpose(
+                        planes[:, t, i * P : (i + 1) * P],
+                        rows_sb[:, first + i, t * P : (t + 1) * P],
+                        ident_bf16[:],
+                    )
+            return planes
+
+        spread = banks.tile([P, K], F32, tag="bank")
+        nc.tensor.matmul(spread[:], lhsT=ones[:], rhs=small_row[:], start=True, stop=True)
+        bias = const.tile([P, HALF], F32)
+        nc.vector.tensor_copy(out=bias[:], in_=spread[:, 0:HALF])
+        dt_plus = const.tile([P, 1], F32)
+        nc.vector.tensor_copy(out=dt_plus[:], in_=spread[:, HALF : HALF + 1])
+        dt_minus = const.tile([P, 1], F32)
+        nc.vector.tensor_scalar_mul(out=dt_minus[:], in0=spread[:, HALF : HALF + 1], scalar1=-1.0)
+
+        w1_grouped = const.tile([P, K, PACK], BF16, align_bytes=64)
+        w1_low = transpose_pair(w1_sb, 0)
+        w1_high = transpose_pair(w1_sb, PAIR)
+        nc.vector.tensor_copy(out=w1_grouped[:, 0:COLS, :], in_=w1_low[:].rearrange("p t c -> p c t"))
+        nc.scalar.copy(out=w1_grouped[:, COLS:K, :], in_=w1_high[:].rearrange("p t c -> p c t"))
+        w1_words = const.tile([P, K], U32, align_bytes=64)
+        w1_scales = const.tile([P, K], U8, align_bytes=64)
+
+        wout_grouped = const.tile([P, HALF, PACK], BF16, align_bytes=64)
+        nc.vector.tensor_copy(out=wout_grouped[:], in_=wout_sb[:].rearrange("p t c -> p c t"))
+        nc.vector.quantize_mx(
+            out=w1_words[:].bitcast(FP8X4),
+            scales=w1_scales[:],
+            in_=w1_grouped[:].rearrange("p c t -> p (c t)"),
+        )
+        wout_words = const.tile([P, HALF], U32, align_bytes=64)
+        wout_scales = const.tile([P, HALF], U8, align_bytes=64)
+        nc.vector.quantize_mx(
+            out=wout_words[:].bitcast(FP8X4),
+            scales=wout_scales[:],
+            in_=wout_grouped[:].rearrange("p c t -> p (c t)"),
+        )
+
+        g1_grouped, g1_mx, state_grouped, state_mx = {}, {}, {}, {}
+        q_new_chunks, p_new_chunks, output_chunks = {}, {}, {}
+
+        def where(n):
+            return (n * PAIR) // CHUNK, (n * PAIR) % CHUNK
+
+        def quantise(grouped, kind):
+            words = work.tile([P, COLS], U32, align_bytes=64, tag=kind + "_words")
+            scales = work.tile([P, COLS], U8, align_bytes=64, tag=kind + "_scales")
+            nc.vector.quantize_mx(
+                out=words[:].bitcast(FP8X4),
+                scales=scales[:],
+                in_=grouped[:].rearrange("p c t -> p (c t)"),
+            )
+            return words, scales
+
+        def multiply(product, stationary, i, moving_words, moving_scales):
+            words, scales = stationary
+            nc.tensor.matmul_mx(
+                out=product[:, i, :],
+                lhsT=words[:, i * P : (i + 1) * P].bitcast(FP8X4),
+                lhsT_scale=scales[:, i * P : (i + 1) * P],
+                rhs=moving_words.bitcast(FP8X4),
+                rhs_scale=moving_scales,
+                start=True,
+                stop=True,
+            )
+
+        def form_g1(n):
+            c, first = where(n)
+            h1_planes = transpose_pair(h1_chunks[c], first)
+            u_planes = transpose_pair(u_chunks[c], first)
+            h1_squared = work.tile([P, COLS, PACK], F32)
+            nc.scalar.activation(
+                out=h1_squared[:], in_=h1_planes[:].rearrange("p t c -> p c t"), func=ACT.Square
+            )
+            grouped = work.tile([P, COLS, PACK], BF16, align_bytes=64, tag="g1_grouped")
+            nc.vector.scalar_tensor_tensor(
+                out=grouped[:],
+                in0=h1_squared[:],
+                scalar=1.0,
+                in1=u_planes[:].rearrange("p t c -> p c t"),
+                op0=ALU.subtract,
+                op1=ALU.mult,
+            )
+            g1_grouped[n] = grouped
+
+        def first_product(n):
+            minus_dh_dp = banks.tile([P, PAIR, HALF], F32, tag="bank")
+            minus_dh_dq = banks.tile([P, PAIR, HALF], F32, tag="bank")
+            for i in range(PAIR):
+                multiply(minus_dh_dp, g1_mx[n], i, w1_words[:, HALF:K], w1_scales[:, HALF:K])
+                multiply(minus_dh_dq, g1_mx[n], i, w1_words[:, 0:HALF], w1_scales[:, 0:HALF])
+            return minus_dh_dp, minus_dh_dq
+
+        def update(n, old_chunks, new_chunks, step_length, gradient):
+            c, first = where(n)
+            nc.vector.scalar_tensor_tensor(
+                out=new_chunks[c][:, first : first + PAIR, :],
+                in0=gradient[:],
+                scalar=step_length[:, 0:1],
+                in1=old_chunks[c][:, first : first + PAIR, :],
+                op0=ALU.mult,
+                op1=ALU.add,
+            )
+
+        def transpose_state(n):
+            c, first = where(n)
+            grouped = work.tile([P, PAIR, P, PACK], BF16, align_bytes=64, tag="state_grouped")
+            for i in range(PAIR):
+                planes = banks.tile([P, PACK, P], F32, tag="bank")
+                for t in range(PACK):
+                    source = q_new_chunks[c] if t * P < HALF else p_new_chunks[c]
+                    column = (t * P) % HALF
+                    nc.tensor.transpose(
+                        planes[:, t, :], source[:, first + i, column : column + P], ident_f32[:]
+                    )
+                nc.scalar.copy(out=grouped[:, i, :, :], in_=planes[:].rearrange("p t r -> p r t"))
+            state_grouped[n] = grouped
+
+        def second_product(n):
+            c, first = where(n)
+            product = banks.tile([P, PAIR, HALF], F32, tag="bank")
+            for i in range(PAIR):
+                multiply(product, state_mx[n], i, wout_words[:], wout_scales[:])
+            nc.vector.tensor_tensor(
+                out=output_chunks[c][:, first : first + PAIR, :],
+                in0=product[:],
+                in1=bias[:].unsqueeze(1).to_broadcast([P, PAIR, HALF]),
+                op=ALU.add,
+            )
+
+        def last_of_chunk(n):
+            return (n + 1) * PAIR % CHUNK == 0
+
+        def in_range(n):
+            return 0 <= n < PAIRS
+
+        def tiles_of_chunk(c):
+            return slice(c * CHUNK, (c + 1) * CHUNK)
+
+        for step in range(PAIRS + 3):
+            pair_a, pair_b, pair_c, pair_d = step, step - 1, step - 2, step - 3
+            if in_range(pair_a):
+                form_g1(pair_a)
+            if in_range(pair_c):
+                transpose_state(pair_c)
+            if in_range(pair_b):
+                c, first = where(pair_b)
+                if first == 0:
+                    q_new_sb = results.tile([P, CHUNK, HALF], F32)
+                    p_new_sb = results.tile([P, CHUNK, HALF], F32)
+                    q_new_chunks[c] = q_new_sb
+                    p_new_chunks[c] = p_new_sb
+                minus_dh_dp, minus_dh_dq = first_product(pair_b)
+                update(pair_b, q_chunks, q_new_chunks, dt_minus, minus_dh_dp)
+            if in_range(pair_a):
+                g1_mx[pair_a] = quantise(g1_grouped[pair_a], "g1")
+            if in_range(pair_b):
+                c, first = where(pair_b)
+                update(pair_b, p_chunks, p_new_chunks, dt_plus, minus_dh_dq)
+                if last_of_chunk(pair_b):
+                    nc.sync.dma_start(out=q_new_rows[:, tiles_of_chunk(c), :], in_=q_new_chunks[c][:])
+                    nc.sync.dma_start(out=p_new_rows[:, tiles_of_chunk(c), :], in_=p_new_chunks[c][:])
+            if in_range(pair_c):
+                state_mx[pair_c] = quantise(state_grouped[pair_c].rearrange("p i r t -> p (i r) t"), "state")
+            if in_range(pair_d):
+                c, first = where(pair_d)
+                if first == 0:
+                    output_sb = results.tile([P, CHUNK, HALF], F32)
+                    output_chunks[c] = output_sb
+                second_product(pair_d)
+                if last_of_chunk(pair_d):
+                    nc.sync.dma_start(out=output_rows[:, tiles_of_chunk(c), :], in_=output_chunks[c][:])

@@ -207,9 +207,11 @@ def tile_timecrystalblock_pb_t_kernel(
             product = banks.tile([P, PAIR, HALF], F32, tag="bank")
             for i in range(PAIR):
                 multiply(product, state_mx[n], i, wout_words[:], wout_scales[:])
-            nc.vector.tensor_tensor(
+            unbiased = work.tile([P, PAIR, HALF], F32)
+            nc.scalar.copy(out=unbiased[:], in_=product[:])
+            nc.gpsimd.tensor_tensor(
                 out=output_chunks[c][:, first : first + PAIR, :],
-                in0=product[:],
+                in0=unbiased[:],
                 in1=bias[:].unsqueeze(1).to_broadcast([P, PAIR, HALF]),
                 op=ALU.add,
             )

@@ -23,6 +23,7 @@ COLS = PAIR * P
 CHUNK = 4
 CHUNKS = TILES // CHUNK
 PSUM_BANKS = 8
+LAG = 2
 
 FLOPS = 2 * BATCH * K * K + 2 * BATCH * K * HALF
 
@@ -129,8 +130,8 @@ def tile_timecrystalblock_pb_t_kernel(
             return (n * PAIR) // CHUNK, (n * PAIR) % CHUNK
 
         def quantise(grouped, kind):
-            words = work.tile([P, COLS], U32, align_bytes=64, tag=kind + "_words")
-            scales = work.tile([P, COLS], U8, align_bytes=64, tag=kind + "_scales")
+            words = work.tile([P, COLS], U32, align_bytes=64, tag=kind + "_words", bufs=LAG + 2)
+            scales = work.tile([P, COLS], U8, align_bytes=64, tag=kind + "_scales", bufs=LAG + 2)
             nc.vector.quantize_mx(
                 out=words[:].bitcast(FP8X4),
                 scales=scales[:],
@@ -174,6 +175,7 @@ def tile_timecrystalblock_pb_t_kernel(
             minus_dh_dq = banks.tile([P, PAIR, HALF], F32, tag="bank")
             for i in range(PAIR):
                 multiply(minus_dh_dp, g1_mx[n], i, w1_words[:, HALF:K], w1_scales[:, HALF:K])
+            for i in range(PAIR):
                 multiply(minus_dh_dq, g1_mx[n], i, w1_words[:, 0:HALF], w1_scales[:, 0:HALF])
             return minus_dh_dp, minus_dh_dq
 
@@ -225,8 +227,8 @@ def tile_timecrystalblock_pb_t_kernel(
         def tiles_of_chunk(c):
             return slice(c * CHUNK, (c + 1) * CHUNK)
 
-        for step in range(PAIRS + 3):
-            pair_a, pair_b, pair_c, pair_d = step, step - 1, step - 2, step - 3
+        for step in range(PAIRS + 3 * LAG):
+            pair_a, pair_b, pair_c, pair_d = step, step - LAG, step - 2 * LAG, step - 3 * LAG
             if in_range(pair_a):
                 form_g1(pair_a)
             if in_range(pair_c):

@@ -24,6 +24,7 @@ CHUNK = 4
 CHUNKS = TILES // CHUNK
 PSUM_BANKS = 8
 LAG = 2
+ADD_PIECE = 128
 
 FLOPS = 2 * BATCH * K * K + 2 * BATCH * K * HALF
 
@@ -60,25 +61,37 @@ def tile_timecrystalblock_pb_t_kernel(
 
         nc.sync.dma_start(out=small_row[0:1, 0:HALF], in_=b_out.unsqueeze(0))
         nc.sync.dma_start(out=small_row[0:1, HALF : HALF + 1], in_=dt.unsqueeze(0))
-        w1_sb = const.tile([P, PACK, K], BF16)
-        nc.sync.dma_start(out=w1_sb[:], in_=W1_qp.rearrange("(a p) k -> p a k", p=P))
         wout_sb = const.tile([P, PACK, HALF], BF16)
         nc.sync.dma_start(out=wout_sb[:], in_=W_out.rearrange("(t p) c -> p t c", p=P))
+        w1_sb = const.tile([P, PACK, K], BF16)
+        nc.sync.dma_start(out=w1_sb[:], in_=W1_qp.rearrange("(a p) k -> p a k", p=P))
         h1_chunks, u_chunks, q_chunks, p_chunks = [], [], [], []
         for c in range(CHUNKS):
-            tiles = slice(c * CHUNK, (c + 1) * CHUNK)
             h1_sb = inputs.tile([P, CHUNK, K], BF16)
-            nc.sync.dma_start(out=h1_sb[:], in_=h1_rows[:, tiles, :])
             u_sb = inputs.tile([P, CHUNK, K], BF16)
-            nc.sync.dma_start(out=u_sb[:], in_=u_rows[:, tiles, :])
             q_sb = inputs.tile([P, CHUNK, HALF], BF16)
-            nc.sync.dma_start(out=q_sb[:], in_=q_rows[:, tiles, :])
             p_sb = inputs.tile([P, CHUNK, HALF], BF16)
-            nc.sync.dma_start(out=p_sb[:], in_=p_rows[:, tiles, :])
             h1_chunks.append(h1_sb)
             u_chunks.append(u_sb)
             q_chunks.append(q_sb)
             p_chunks.append(p_sb)
+
+        def load(rows, chunks, c, first, count):
+            tile_0 = c * CHUNK + first
+            nc.sync.dma_start(
+                out=chunks[c][:, first : first + count, :], in_=rows[:, tile_0 : tile_0 + count, :]
+            )
+
+        for first in range(0, CHUNK, PAIR):
+            load(h1_rows, h1_chunks, 0, first, PAIR)
+            load(u_rows, u_chunks, 0, first, PAIR)
+        load(q_rows, q_chunks, 0, 0, CHUNK)
+        load(p_rows, p_chunks, 0, 0, CHUNK)
+        for c in range(1, CHUNKS):
+            load(h1_rows, h1_chunks, c, 0, CHUNK)
+            load(u_rows, u_chunks, c, 0, CHUNK)
+            load(q_rows, q_chunks, c, 0, CHUNK)
+            load(p_rows, p_chunks, c, 0, CHUNK)
 
         def transpose_pair(rows_sb, first):
             planes = banks.tile([P, PACK, COLS], BF16, tag="bank")
@@ -91,36 +104,39 @@ def tile_timecrystalblock_pb_t_kernel(
                     )
             return planes
 
+        wout_grouped = const.tile([P, HALF, PACK], BF16, align_bytes=64)
+        nc.vector.tensor_copy(out=wout_grouped[:], in_=wout_sb[:].rearrange("p t c -> p c t"))
+
         spread = banks.tile([P, K], F32, tag="bank")
         nc.tensor.matmul(spread[:], lhsT=ones[:], rhs=small_row[:], start=True, stop=True)
-        bias = const.tile([P, HALF], F32)
-        nc.vector.tensor_copy(out=bias[:], in_=spread[:, 0:HALF])
+        bias = const.tile([P, PAIR, HALF], F32)
+        nc.vector.tensor_copy(
+            out=bias[:], in_=spread[:, 0:HALF].unsqueeze(1).to_broadcast([P, PAIR, HALF])
+        )
         dt_plus = const.tile([P, 1], F32)
         nc.vector.tensor_copy(out=dt_plus[:], in_=spread[:, HALF : HALF + 1])
         dt_minus = const.tile([P, 1], F32)
         nc.vector.tensor_scalar_mul(out=dt_minus[:], in0=spread[:, HALF : HALF + 1], scalar1=-1.0)
 
-        w1_grouped = const.tile([P, K, PACK], BF16, align_bytes=64)
-        w1_low = transpose_pair(w1_sb, 0)
-        w1_high = transpose_pair(w1_sb, PAIR)
-        nc.vector.tensor_copy(out=w1_grouped[:, 0:COLS, :], in_=w1_low[:].rearrange("p t c -> p c t"))
-        nc.scalar.copy(out=w1_grouped[:, COLS:K, :], in_=w1_high[:].rearrange("p t c -> p c t"))
-        w1_words = const.tile([P, K], U32, align_bytes=64)
-        w1_scales = const.tile([P, K], U8, align_bytes=64)
-
-        wout_grouped = const.tile([P, HALF, PACK], BF16, align_bytes=64)
-        nc.vector.tensor_copy(out=wout_grouped[:], in_=wout_sb[:].rearrange("p t c -> p c t"))
-        nc.vector.quantize_mx(
-            out=w1_words[:].bitcast(FP8X4),
-            scales=w1_scales[:],
-            in_=w1_grouped[:].rearrange("p c t -> p (c t)"),
-        )
         wout_words = const.tile([P, HALF], U32, align_bytes=64)
         wout_scales = const.tile([P, HALF], U8, align_bytes=64)
         nc.vector.quantize_mx(
             out=wout_words[:].bitcast(FP8X4),
             scales=wout_scales[:],
             in_=wout_grouped[:].rearrange("p c t -> p (c t)"),
+        )
+
+        w1_grouped = const.tile([P, K, PACK], BF16, align_bytes=64)
+        w1_low = transpose_pair(w1_sb, 0)
+        w1_high = transpose_pair(w1_sb, PAIR)
+        nc.vector.tensor_copy(out=w1_grouped[:, 0:COLS, :], in_=w1_low[:].rearrange("p t c -> p c t"))
+        nc.vector.tensor_copy(out=w1_grouped[:, COLS:K, :], in_=w1_high[:].rearrange("p t c -> p c t"))
+        w1_words = const.tile([P, K], U32, align_bytes=64)
+        w1_scales = const.tile([P, K], U8, align_bytes=64)
+        nc.vector.quantize_mx(
+            out=w1_words[:].bitcast(FP8X4),
+            scales=w1_scales[:],
+            in_=w1_grouped[:].rearrange("p c t -> p (c t)"),
         )
 
         g1_grouped, g1_mx, state_grouped, state_mx = {}, {}, {}, {}
@@ -204,19 +220,23 @@ def tile_timecrystalblock_pb_t_kernel(
                 nc.scalar.copy(out=grouped[:, i, :, :], in_=planes[:].rearrange("p t r -> p r t"))
             state_grouped[n] = grouped
 
-        def second_product(n):
+        def second_product(n, vector_is_free):
             c, first = where(n)
             product = banks.tile([P, PAIR, HALF], F32, tag="bank")
             for i in range(PAIR):
                 multiply(product, state_mx[n], i, wout_words[:], wout_scales[:])
-            unbiased = work.tile([P, PAIR, HALF], F32)
-            nc.scalar.copy(out=unbiased[:], in_=product[:])
-            nc.gpsimd.tensor_tensor(
-                out=output_chunks[c][:, first : first + PAIR, :],
-                in0=unbiased[:],
-                in1=bias[:].unsqueeze(1).to_broadcast([P, PAIR, HALF]),
-                op=ALU.add,
-            )
+            output_pair = output_chunks[c][:, first : first + PAIR, :]
+            if vector_is_free:
+                nc.vector.tensor_tensor(out=output_pair, in0=product[:], in1=bias[:], op=ALU.add)
+            else:
+                unbiased = work.tile([P, PAIR, HALF], F32)
+                nc.scalar.copy(out=unbiased[:], in_=product[:])
+                for i in range(PAIR):
+                    for start in range(0, HALF, ADD_PIECE):
+                        piece = slice(start, start + ADD_PIECE)
+                        nc.gpsimd.tensor_tensor(
+                            out=output_pair[:, i, piece], in0=unbiased[:, i, piece], in1=bias[:, i, piece], op=ALU.add
+                        )
 
         def last_of_chunk(n):
             return (n + 1) * PAIR % CHUNK == 0
@@ -257,6 +277,6 @@ def tile_timecrystalblock_pb_t_kernel(
                 if first == 0:
                     output_sb = results.tile([P, CHUNK, HALF], F32)
                     output_chunks[c] = output_sb
-                second_product(pair_d)
+                second_product(pair_d, vector_is_free=pair_b >= PAIRS)
                 if last_of_chunk(pair_d):
                     nc.sync.dma_start(out=output_rows[:, tiles_of_chunk(c), :], in_=output_chunks[c][:])

@@ -64,7 +64,9 @@ def tile_timecrystalblock_pb_t_kernel(
         wout_sb = const.tile([P, PACK, HALF], BF16)
         nc.sync.dma_start(out=wout_sb[:], in_=W_out.rearrange("(t p) c -> p t c", p=P))
         w1_sb = const.tile([P, PACK, K], BF16)
-        nc.sync.dma_start(out=w1_sb[:], in_=W1_qp.rearrange("(a p) k -> p a k", p=P))
+        w1_rows = W1_qp.rearrange("(a p) k -> p a k", p=P)
+        for first in range(0, PACK, PAIR):
+            nc.sync.dma_start(out=w1_sb[:, first : first + PAIR, :], in_=w1_rows[:, first : first + PAIR, :])
         h1_chunks, u_chunks, q_chunks, p_chunks = [], [], [], []
         for c in range(CHUNKS):
             h1_sb = inputs.tile([P, CHUNK, K], BF16)
@@ -140,7 +142,7 @@ def tile_timecrystalblock_pb_t_kernel(
         )
 
         g1_grouped, g1_mx, state_grouped, state_mx = {}, {}, {}, {}
-        q_new_chunks, p_new_chunks, output_chunks = {}, {}, {}
+        q_new_chunks, p_new_chunks = {}, {}
 
         def where(n):
             return (n * PAIR) // CHUNK, (n * PAIR) % CHUNK
@@ -206,7 +208,7 @@ def tile_timecrystalblock_pb_t_kernel(
                 op1=ALU.add,
             )
 
-        def transpose_state(n):
+        def transpose_state(n, share_copies):
             c, first = where(n)
             grouped = work.tile([P, PAIR, P, PACK], BF16, align_bytes=64, tag="state_grouped")
             for i in range(PAIR):
@@ -217,17 +219,19 @@ def tile_timecrystalblock_pb_t_kernel(
                     nc.tensor.transpose(
                         planes[:, t, :], source[:, first + i, column : column + P], ident_f32[:]
                     )
-                nc.scalar.copy(out=grouped[:, i, :, :], in_=planes[:].rearrange("p t r -> p r t"))
+                if share_copies and i == 1:
+                    nc.vector.tensor_copy(out=grouped[:, i, :, :], in_=planes[:].rearrange("p t r -> p r t"))
+                else:
+                    nc.scalar.copy(out=grouped[:, i, :, :], in_=planes[:].rearrange("p t r -> p r t"))
             state_grouped[n] = grouped
 
-        def second_product(n, vector_is_free):
-            c, first = where(n)
+        def second_product(n, on_vector):
             product = banks.tile([P, PAIR, HALF], F32, tag="bank")
             for i in range(PAIR):
                 multiply(product, state_mx[n], i, wout_words[:], wout_scales[:])
-            output_pair = output_chunks[c][:, first : first + PAIR, :]
-            if vector_is_free:
-                nc.vector.tensor_tensor(out=output_pair, in0=product[:], in1=bias[:], op=ALU.add)
+            output_pair = results.tile([P, PAIR, HALF], F32)
+            if on_vector:
+                nc.vector.tensor_tensor(out=output_pair[:], in0=product[:], in1=bias[:], op=ALU.add)
             else:
                 unbiased = work.tile([P, PAIR, HALF], F32)
                 nc.scalar.copy(out=unbiased[:], in_=product[:])
@@ -237,6 +241,7 @@ def tile_timecrystalblock_pb_t_kernel(
                         nc.gpsimd.tensor_tensor(
                             out=output_pair[:, i, piece], in0=unbiased[:, i, piece], in1=bias[:, i, piece], op=ALU.add
                         )
+            nc.sync.dma_start(out=output_rows[:, n * PAIR : (n + 1) * PAIR, :], in_=output_pair[:])
 
         def last_of_chunk(n):
             return (n + 1) * PAIR % CHUNK == 0
@@ -249,10 +254,11 @@ def tile_timecrystalblock_pb_t_kernel(
 
         for step in range(PAIRS + 3 * LAG):
             pair_a, pair_b, pair_c, pair_d = step, step - LAG, step - 2 * LAG, step - 3 * LAG
+            vector_is_free = pair_b >= PAIRS
             if in_range(pair_a):
                 form_g1(pair_a)
             if in_range(pair_c):
-                transpose_state(pair_c)
+                transpose_state(pair_c, share_copies=vector_is_free)
             if in_range(pair_b):
                 c, first = where(pair_b)
                 if first == 0:
@@ -273,10 +279,4 @@ def tile_timecrystalblock_pb_t_kernel(
             if in_range(pair_c):
                 state_mx[pair_c] = quantise(state_grouped[pair_c].rearrange("p i r t -> p (i r) t"), "state")
             if in_range(pair_d):
-                c, first = where(pair_d)
-                if first == 0:
-                    output_sb = results.tile([P, CHUNK, HALF], F32)
-                    output_chunks[c] = output_sb
-                second_product(pair_d, vector_is_free=pair_b >= PAIRS)
-                if last_of_chunk(pair_d):
-                    nc.sync.dma_start(out=output_rows[:, tiles_of_chunk(c), :], in_=output_chunks[c][:])
+                second_product(pair_d, on_vector=vector_is_free or pair_d % 2 == 1)

@@ -64,9 +64,7 @@ def tile_timecrystalblock_pb_t_kernel(
         wout_sb = const.tile([P, PACK, HALF], BF16)
         nc.sync.dma_start(out=wout_sb[:], in_=W_out.rearrange("(t p) c -> p t c", p=P))
         w1_sb = const.tile([P, PACK, K], BF16)
-        w1_rows = W1_qp.rearrange("(a p) k -> p a k", p=P)
-        for first in range(0, PACK, PAIR):
-            nc.sync.dma_start(out=w1_sb[:, first : first + PAIR, :], in_=w1_rows[:, first : first + PAIR, :])
+        nc.sync.dma_start(out=w1_sb[:], in_=W1_qp.rearrange("(a p) k -> p a k", p=P))
         h1_chunks, u_chunks, q_chunks, p_chunks = [], [], [], []
         for c in range(CHUNKS):
             h1_sb = inputs.tile([P, CHUNK, K], BF16)
@@ -141,8 +139,8 @@ def tile_timecrystalblock_pb_t_kernel(
             in_=w1_grouped[:].rearrange("p c t -> p (c t)"),
         )
 
-        g1_grouped, g1_mx, state_grouped, state_mx = {}, {}, {}, {}
-        q_new_chunks, p_new_chunks = {}, {}
+        h1_squared, g1_grouped, g1_mx, state_grouped, state_mx = {}, {}, {}, {}, {}
+        q_new_chunks, p_new_chunks, output_chunks = {}, {}, {}
 
         def where(n):
             return (n * PAIR) // CHUNK, (n * PAIR) % CHUNK
@@ -169,18 +167,20 @@ def tile_timecrystalblock_pb_t_kernel(
                 stop=True,
             )
 
-        def form_g1(n):
+        def square_h1(n):
             c, first = where(n)
             h1_planes = transpose_pair(h1_chunks[c], first)
+            squared = work.tile([P, COLS, PACK], F32, tag="h1_squared", bufs=3)
+            nc.scalar.activation(out=squared[:], in_=h1_planes[:].rearrange("p t c -> p c t"), func=ACT.Square)
+            h1_squared[n] = squared
+
+        def form_g1(n):
+            c, first = where(n)
             u_planes = transpose_pair(u_chunks[c], first)
-            h1_squared = work.tile([P, COLS, PACK], F32)
-            nc.scalar.activation(
-                out=h1_squared[:], in_=h1_planes[:].rearrange("p t c -> p c t"), func=ACT.Square
-            )
             grouped = work.tile([P, COLS, PACK], BF16, align_bytes=64, tag="g1_grouped")
             nc.vector.scalar_tensor_tensor(
                 out=grouped[:],
-                in0=h1_squared[:],
+                in0=h1_squared[n][:],
                 scalar=1.0,
                 in1=u_planes[:].rearrange("p t c -> p c t"),
                 op0=ALU.subtract,
@@ -208,7 +208,7 @@ def tile_timecrystalblock_pb_t_kernel(
                 op1=ALU.add,
             )
 
-        def transpose_state(n, share_copies):
+        def transpose_state(n):
             c, first = where(n)
             grouped = work.tile([P, PAIR, P, PACK], BF16, align_bytes=64, tag="state_grouped")
             for i in range(PAIR):
@@ -219,19 +219,17 @@ def tile_timecrystalblock_pb_t_kernel(
                     nc.tensor.transpose(
                         planes[:, t, :], source[:, first + i, column : column + P], ident_f32[:]
                     )
-                if share_copies and i == 1:
-                    nc.vector.tensor_copy(out=grouped[:, i, :, :], in_=planes[:].rearrange("p t r -> p r t"))
-                else:
-                    nc.scalar.copy(out=grouped[:, i, :, :], in_=planes[:].rearrange("p t r -> p r t"))
+                nc.scalar.copy(out=grouped[:, i, :, :], in_=planes[:].rearrange("p t r -> p r t"))
             state_grouped[n] = grouped
 
-        def second_product(n, on_vector):
+        def second_product(n, vector_is_free):
+            c, first = where(n)
             product = banks.tile([P, PAIR, HALF], F32, tag="bank")
             for i in range(PAIR):
                 multiply(product, state_mx[n], i, wout_words[:], wout_scales[:])
-            output_pair = results.tile([P, PAIR, HALF], F32)
-            if on_vector:
-                nc.vector.tensor_tensor(out=output_pair[:], in0=product[:], in1=bias[:], op=ALU.add)
+            output_pair = output_chunks[c][:, first : first + PAIR, :]
+            if vector_is_free:
+                nc.vector.tensor_tensor(out=output_pair, in0=product[:], in1=bias[:], op=ALU.add)
             else:
                 unbiased = work.tile([P, PAIR, HALF], F32)
                 nc.scalar.copy(out=unbiased[:], in_=product[:])
@@ -241,7 +239,6 @@ def tile_timecrystalblock_pb_t_kernel(
                         nc.gpsimd.tensor_tensor(
                             out=output_pair[:, i, piece], in0=unbiased[:, i, piece], in1=bias[:, i, piece], op=ALU.add
                         )
-            nc.sync.dma_start(out=output_rows[:, n * PAIR : (n + 1) * PAIR, :], in_=output_pair[:])
 
         def last_of_chunk(n):
             return (n + 1) * PAIR % CHUNK == 0
@@ -252,31 +249,39 @@ def tile_timecrystalblock_pb_t_kernel(
         def tiles_of_chunk(c):
             return slice(c * CHUNK, (c + 1) * CHUNK)
 
-        for step in range(PAIRS + 3 * LAG):
-            pair_a, pair_b, pair_c, pair_d = step, step - LAG, step - 2 * LAG, step - 3 * LAG
-            vector_is_free = pair_b >= PAIRS
+        for step in range(PAIRS + 1 + 3 * LAG):
+            pair_a, pair_b = step, step - 1
+            pair_c, pair_d, pair_e = pair_b - LAG, pair_b - 2 * LAG, pair_b - 3 * LAG
             if in_range(pair_a):
-                form_g1(pair_a)
-            if in_range(pair_c):
-                transpose_state(pair_c, share_copies=vector_is_free)
+                square_h1(pair_a)
             if in_range(pair_b):
-                c, first = where(pair_b)
+                form_g1(pair_b)
+            if in_range(pair_d):
+                transpose_state(pair_d)
+            if in_range(pair_c):
+                c, first = where(pair_c)
                 if first == 0:
                     q_new_sb = results.tile([P, CHUNK, HALF], F32)
                     p_new_sb = results.tile([P, CHUNK, HALF], F32)
                     q_new_chunks[c] = q_new_sb
                     p_new_chunks[c] = p_new_sb
-                minus_dh_dp, minus_dh_dq = first_product(pair_b)
-                update(pair_b, q_chunks, q_new_chunks, dt_minus, minus_dh_dp)
-            if in_range(pair_a):
-                g1_mx[pair_a] = quantise(g1_grouped[pair_a], "g1")
+                minus_dh_dp, minus_dh_dq = first_product(pair_c)
+                update(pair_c, q_chunks, q_new_chunks, dt_minus, minus_dh_dp)
             if in_range(pair_b):
-                c, first = where(pair_b)
-                update(pair_b, p_chunks, p_new_chunks, dt_plus, minus_dh_dq)
-                if last_of_chunk(pair_b):
+                g1_mx[pair_b] = quantise(g1_grouped[pair_b], "g1")
+            if in_range(pair_c):
+                c, first = where(pair_c)
+                update(pair_c, p_chunks, p_new_chunks, dt_plus, minus_dh_dq)
+                if last_of_chunk(pair_c):
                     nc.sync.dma_start(out=q_new_rows[:, tiles_of_chunk(c), :], in_=q_new_chunks[c][:])
                     nc.sync.dma_start(out=p_new_rows[:, tiles_of_chunk(c), :], in_=p_new_chunks[c][:])
-            if in_range(pair_c):
-                state_mx[pair_c] = quantise(state_grouped[pair_c].rearrange("p i r t -> p (i r) t"), "state")
             if in_range(pair_d):
-                second_product(pair_d, on_vector=vector_is_free or pair_d % 2 == 1)
+                state_mx[pair_d] = quantise(state_grouped[pair_d].rearrange("p i r t -> p (i r) t"), "state")
+            if in_range(pair_e):
+                c, first = where(pair_e)
+                if first == 0:
+                    output_sb = results.tile([P, CHUNK, HALF], F32)
+                    output_chunks[c] = output_sb
+                second_product(pair_e, vector_is_free=pair_c >= PAIRS)
+                if last_of_chunk(pair_e):
+                    nc.sync.dma_start(out=output_rows[:, tiles_of_chunk(c), :], in_=output_chunks[c][:])

@@ -55,16 +55,10 @@ def tile_timecrystalblock_pb_t_kernel(
         ident_f32 = const.tile([P, P], F32)
         make_identity(nc, ident_f32[:])
         ones = const.tile([P, P], BF16)
-        nc.vector.memset(ones[:], 1.0)
+        nc.gpsimd.memset(ones[:], 1.0)
         small_row = const.tile([P, K], BF16)
-        nc.vector.memset(small_row[:], 0.0)
+        nc.gpsimd.memset(small_row[:], 0.0)
 
-        nc.sync.dma_start(out=small_row[0:1, 0:HALF], in_=b_out.unsqueeze(0))
-        nc.sync.dma_start(out=small_row[0:1, HALF : HALF + 1], in_=dt.unsqueeze(0))
-        wout_sb = const.tile([P, PACK, HALF], BF16)
-        nc.sync.dma_start(out=wout_sb[:], in_=W_out.rearrange("(t p) c -> p t c", p=P))
-        w1_sb = const.tile([P, PACK, K], BF16)
-        nc.sync.dma_start(out=w1_sb[:], in_=W1_qp.rearrange("(a p) k -> p a k", p=P))
         h1_chunks, u_chunks, q_chunks, p_chunks = [], [], [], []
         for c in range(CHUNKS):
             h1_sb = inputs.tile([P, CHUNK, K], BF16)
@@ -82,12 +76,29 @@ def tile_timecrystalblock_pb_t_kernel(
                 out=chunks[c][:, first : first + count, :], in_=rows[:, tile_0 : tile_0 + count, :]
             )
 
-        for first in range(0, CHUNK, PAIR):
-            load(h1_rows, h1_chunks, 0, first, PAIR)
-            load(u_rows, u_chunks, 0, first, PAIR)
+        wout_sb = const.tile([P, PACK, HALF], BF16)
+        w1_sb = const.tile([P, PACK, K], BF16)
+        load(h1_rows, h1_chunks, 0, 0, PAIR)
+        load(u_rows, u_chunks, 0, 0, PAIR)
+        load(h1_rows, h1_chunks, 0, PAIR, PAIR)
+        load(u_rows, u_chunks, 0, PAIR, PAIR)
+        load(h1_rows, h1_chunks, 1, 0, PAIR)
+        nc.sync.dma_start(out=w1_sb[:], in_=W1_qp.rearrange("(a p) k -> p a k", p=P))
+        nc.sync.dma_start(out=small_row[0:1, 0:HALF], in_=b_out.unsqueeze(0))
+        nc.sync.dma_start(out=small_row[0:1, HALF : HALF + 1], in_=dt.unsqueeze(0))
+        load(h1_rows, h1_chunks, 1, PAIR, PAIR)
+        load(u_rows, u_chunks, 1, 0, PAIR)
         load(q_rows, q_chunks, 0, 0, CHUNK)
         load(p_rows, p_chunks, 0, 0, CHUNK)
-        for c in range(1, CHUNKS):
+        load(u_rows, u_chunks, 1, PAIR, PAIR)
+        nc.sync.dma_start(out=wout_sb[:], in_=W_out.rearrange("(t p) c -> p t c", p=P))
+        load(h1_rows, h1_chunks, 2, 0, CHUNK)
+        load(u_rows, u_chunks, 2, 0, CHUNK)
+        load(q_rows, q_chunks, 1, 0, CHUNK)
+        load(p_rows, p_chunks, 1, 0, CHUNK)
+        load(q_rows, q_chunks, 2, 0, CHUNK)
+        load(p_rows, p_chunks, 2, 0, CHUNK)
+        for c in range(3, CHUNKS):
             load(h1_rows, h1_chunks, c, 0, CHUNK)
             load(u_rows, u_chunks, c, 0, CHUNK)
             load(q_rows, q_chunks, c, 0, CHUNK)
@@ -105,39 +116,51 @@ def tile_timecrystalblock_pb_t_kernel(
             return planes
 
         wout_grouped = const.tile([P, HALF, PACK], BF16, align_bytes=64)
-        nc.vector.tensor_copy(out=wout_grouped[:], in_=wout_sb[:].rearrange("p t c -> p c t"))
-
-        spread = banks.tile([P, K], F32, tag="bank")
-        nc.tensor.matmul(spread[:], lhsT=ones[:], rhs=small_row[:], start=True, stop=True)
-        bias = const.tile([P, PAIR, HALF], F32)
-        nc.vector.tensor_copy(
-            out=bias[:], in_=spread[:, 0:HALF].unsqueeze(1).to_broadcast([P, PAIR, HALF])
-        )
-        dt_plus = const.tile([P, 1], F32)
-        nc.vector.tensor_copy(out=dt_plus[:], in_=spread[:, HALF : HALF + 1])
-        dt_minus = const.tile([P, 1], F32)
-        nc.vector.tensor_scalar_mul(out=dt_minus[:], in0=spread[:, HALF : HALF + 1], scalar1=-1.0)
-
         wout_words = const.tile([P, HALF], U32, align_bytes=64)
         wout_scales = const.tile([P, HALF], U8, align_bytes=64)
-        nc.vector.quantize_mx(
-            out=wout_words[:].bitcast(FP8X4),
-            scales=wout_scales[:],
-            in_=wout_grouped[:].rearrange("p c t -> p (c t)"),
-        )
-
         w1_grouped = const.tile([P, K, PACK], BF16, align_bytes=64)
-        w1_low = transpose_pair(w1_sb, 0)
-        w1_high = transpose_pair(w1_sb, PAIR)
-        nc.vector.tensor_copy(out=w1_grouped[:, 0:COLS, :], in_=w1_low[:].rearrange("p t c -> p c t"))
-        nc.vector.tensor_copy(out=w1_grouped[:, COLS:K, :], in_=w1_high[:].rearrange("p t c -> p c t"))
         w1_words = const.tile([P, K], U32, align_bytes=64)
         w1_scales = const.tile([P, K], U8, align_bytes=64)
-        nc.vector.quantize_mx(
-            out=w1_words[:].bitcast(FP8X4),
-            scales=w1_scales[:],
-            in_=w1_grouped[:].rearrange("p c t -> p (c t)"),
-        )
+        bias = const.tile([P, PAIR, HALF], F32)
+        dt_plus = const.tile([P, 1], F32)
+        dt_minus = const.tile([P, 1], F32)
+
+        def transpose_w1():
+            w1_low = transpose_pair(w1_sb, 0)
+            w1_high = transpose_pair(w1_sb, PAIR)
+            nc.scalar.copy(out=w1_grouped[:, 0:COLS, :], in_=w1_low[:].rearrange("p t c -> p c t"))
+            nc.vector.tensor_copy(out=w1_grouped[:, COLS:K, :], in_=w1_high[:].rearrange("p t c -> p c t"))
+
+        def quantise_w1():
+            nc.vector.quantize_mx(
+                out=w1_words[:].bitcast(FP8X4),
+                scales=w1_scales[:],
+                in_=w1_grouped[:].rearrange("p c t -> p (c t)"),
+            )
+
+        def spread_small_row():
+            spread = banks.tile([P, K], F32, tag="bank")
+            nc.tensor.matmul(spread[:], lhsT=ones[:], rhs=small_row[:], start=True, stop=True)
+            nc.scalar.copy(out=dt_plus[:], in_=spread[:, HALF : HALF + 1])
+            nc.scalar.mul(dt_minus[:], spread[:, HALF : HALF + 1], -1.0)
+            nc.scalar.copy(out=bias[:], in_=spread[:, 0:HALF].unsqueeze(1).to_broadcast([P, PAIR, HALF]))
+
+        def group_wout():
+            nc.gpsimd.tensor_scalar(
+                out=wout_grouped[:],
+                in0=wout_sb[:].rearrange("p t c -> p c t"),
+                scalar1=1.0,
+                scalar2=0.0,
+                op0=ALU.mult,
+                op1=ALU.add,
+            )
+
+        def quantise_wout():
+            nc.vector.quantize_mx(
+                out=wout_words[:].bitcast(FP8X4),
+                scales=wout_scales[:],
+                in_=wout_grouped[:].rearrange("p c t -> p (c t)"),
+            )
 
         h1_squared, g1_grouped, g1_mx, state_grouped, state_mx = {}, {}, {}, {}, {}
         q_new_chunks, p_new_chunks, output_chunks = {}, {}, {}
@@ -252,10 +275,17 @@ def tile_timecrystalblock_pb_t_kernel(
         for step in range(PAIRS + 1 + 3 * LAG):
             pair_a, pair_b = step, step - 1
             pair_c, pair_d, pair_e = pair_b - LAG, pair_b - 2 * LAG, pair_b - 3 * LAG
-            if in_range(pair_a):
-                square_h1(pair_a)
+            if pair_c == 0:
+                quantise_w1()
             if in_range(pair_b):
                 form_g1(pair_b)
+            if in_range(pair_a):
+                square_h1(pair_a)
+            if pair_c == -1:
+                transpose_w1()
+                spread_small_row()
+            if pair_d == -1:
+                group_wout()
             if in_range(pair_d):
                 transpose_state(pair_d)
             if in_range(pair_c):
@@ -277,6 +307,8 @@ def tile_timecrystalblock_pb_t_kernel(
                     nc.sync.dma_start(out=p_new_rows[:, tiles_of_chunk(c), :], in_=p_new_chunks[c][:])
             if in_range(pair_d):
                 state_mx[pair_d] = quantise(state_grouped[pair_d].rearrange("p i r t -> p (i r) t"), "state")
+            if pair_e == -1:
+                quantise_wout()
             if in_range(pair_e):
                 c, first = where(pair_e)
                 if first == 0:

@@ -129,7 +129,7 @@ def tile_timecrystalblock_pb_t_kernel(
             w1_low = transpose_pair(w1_sb, 0)
             w1_high = transpose_pair(w1_sb, PAIR)
             nc.scalar.copy(out=w1_grouped[:, 0:COLS, :], in_=w1_low[:].rearrange("p t c -> p c t"))
-            nc.vector.tensor_copy(out=w1_grouped[:, COLS:K, :], in_=w1_high[:].rearrange("p t c -> p c t"))
+            nc.scalar.copy(out=w1_grouped[:, COLS:K, :], in_=w1_high[:].rearrange("p t c -> p c t"))
 
         def quantise_w1():
             nc.vector.quantize_mx(
@@ -162,21 +162,22 @@ def tile_timecrystalblock_pb_t_kernel(
                 in_=wout_grouped[:].rearrange("p c t -> p (c t)"),
             )
 
-        h1_squared, g1_grouped, g1_mx, state_grouped, state_mx = {}, {}, {}, {}, {}
+        h1_squared, g1_mx, state_mx = {}, {}, {}
         q_new_chunks, p_new_chunks, output_chunks = {}, {}, {}
 
         def where(n):
             return (n * PAIR) // CHUNK, (n * PAIR) % CHUNK
 
-        def quantise(grouped, kind):
-            words = work.tile([P, COLS], U32, align_bytes=64, tag=kind + "_words", bufs=LAG + 2)
-            scales = work.tile([P, COLS], U8, align_bytes=64, tag=kind + "_scales", bufs=LAG + 2)
+        def quantise(values, has_g1, has_state):
+            words = work.tile([P, 2, COLS], U32, align_bytes=64, tag="words", bufs=LAG + 2)
+            scales = work.tile([P, 2, COLS], U8, align_bytes=64, tag="scales", bufs=LAG + 2)
+            halves = slice(0 if has_g1 else 1, 2 if has_state else 1)
             nc.vector.quantize_mx(
-                out=words[:].bitcast(FP8X4),
-                scales=scales[:],
-                in_=grouped[:].rearrange("p c t -> p (c t)"),
+                out=words[:, halves, :].rearrange("p h c -> p (h c)").bitcast(FP8X4),
+                scales=scales[:, halves, :].rearrange("p h c -> p (h c)"),
+                in_=values[:, halves, :, :].rearrange("p h c t -> p (h c t)"),
             )
-            return words, scales
+            return [(words[:, h, :], scales[:, h, :]) for h in range(2)]
 
         def multiply(product, stationary, i, moving_words, moving_scales):
             words, scales = stationary
@@ -197,19 +198,17 @@ def tile_timecrystalblock_pb_t_kernel(
             nc.scalar.activation(out=squared[:], in_=h1_planes[:].rearrange("p t c -> p c t"), func=ACT.Square)
             h1_squared[n] = squared
 
-        def form_g1(n):
+        def form_g1(n, values):
             c, first = where(n)
             u_planes = transpose_pair(u_chunks[c], first)
-            grouped = work.tile([P, COLS, PACK], BF16, align_bytes=64, tag="g1_grouped")
             nc.vector.scalar_tensor_tensor(
-                out=grouped[:],
+                out=values[:, 0, :, :],
                 in0=h1_squared[n][:],
                 scalar=1.0,
                 in1=u_planes[:].rearrange("p t c -> p c t"),
                 op0=ALU.subtract,
                 op1=ALU.mult,
             )
-            g1_grouped[n] = grouped
 
         def first_product(n):
             minus_dh_dp = banks.tile([P, PAIR, HALF], F32, tag="bank")
@@ -231,9 +230,8 @@ def tile_timecrystalblock_pb_t_kernel(
                 op1=ALU.add,
             )
 
-        def transpose_state(n):
+        def transpose_state(n, values):
             c, first = where(n)
-            grouped = work.tile([P, PAIR, P, PACK], BF16, align_bytes=64, tag="state_grouped")
             for i in range(PAIR):
                 planes = banks.tile([P, PACK, P], F32, tag="bank")
                 for t in range(PACK):
@@ -242,8 +240,7 @@ def tile_timecrystalblock_pb_t_kernel(
                     nc.tensor.transpose(
                         planes[:, t, :], source[:, first + i, column : column + P], ident_f32[:]
                     )
-                nc.scalar.copy(out=grouped[:, i, :, :], in_=planes[:].rearrange("p t r -> p r t"))
-            state_grouped[n] = grouped
+                nc.scalar.copy(out=values[:, 1, i * P : (i + 1) * P, :], in_=planes[:].rearrange("p t r -> p r t"))
 
         def second_product(n, vector_is_free):
             c, first = where(n)
@@ -277,8 +274,10 @@ def tile_timecrystalblock_pb_t_kernel(
             pair_c, pair_d, pair_e = pair_b - LAG, pair_b - 2 * LAG, pair_b - 3 * LAG
             if pair_c == 0:
                 quantise_w1()
+            if in_range(pair_b) or in_range(pair_d):
+                values = work.tile([P, 2, COLS, PACK], BF16, align_bytes=64)
             if in_range(pair_b):
-                form_g1(pair_b)
+                form_g1(pair_b, values)
             if in_range(pair_a):
                 square_h1(pair_a)
             if pair_c == -1:
@@ -287,7 +286,7 @@ def tile_timecrystalblock_pb_t_kernel(
             if pair_d == -1:
                 group_wout()
             if in_range(pair_d):
-                transpose_state(pair_d)
+                transpose_state(pair_d, values)
             if in_range(pair_c):
                 c, first = where(pair_c)
                 if first == 0:
@@ -297,16 +296,12 @@ def tile_timecrystalblock_pb_t_kernel(
                     p_new_chunks[c] = p_new_sb
                 minus_dh_dp, minus_dh_dq = first_product(pair_c)
                 update(pair_c, q_chunks, q_new_chunks, dt_minus, minus_dh_dp)
-            if in_range(pair_b):
-                g1_mx[pair_b] = quantise(g1_grouped[pair_b], "g1")
-            if in_range(pair_c):
-                c, first = where(pair_c)
                 update(pair_c, p_chunks, p_new_chunks, dt_plus, minus_dh_dq)
                 if last_of_chunk(pair_c):
                     nc.sync.dma_start(out=q_new_rows[:, tiles_of_chunk(c), :], in_=q_new_chunks[c][:])
                     nc.sync.dma_start(out=p_new_rows[:, tiles_of_chunk(c), :], in_=p_new_chunks[c][:])
-            if in_range(pair_d):
-                state_mx[pair_d] = quantise(state_grouped[pair_d].rearrange("p i r t -> p (i r) t"), "state")
+            if in_range(pair_b) or in_range(pair_d):
+                g1_mx[pair_b], state_mx[pair_d] = quantise(values, in_range(pair_b), in_range(pair_d))
             if pair_e == -1:
                 quantise_wout()
             if in_range(pair_e):

@@ -52,10 +52,10 @@ def tile_timecrystalblock_pb_t_kernel(
 
         ident_bf16 = const.tile([P, P], BF16)
         make_identity(nc, ident_bf16[:])
+        ones = const.tile([P, K], BF16)
+        nc.vector.memset(ones[:], 1.0)
         ident_f32 = const.tile([P, P], F32)
         make_identity(nc, ident_f32[:])
-        ones = const.tile([P, P], BF16)
-        nc.gpsimd.memset(ones[:], 1.0)
         small_row = const.tile([P, K], BF16)
         nc.gpsimd.memset(small_row[:], 0.0)
 
@@ -140,7 +140,7 @@ def tile_timecrystalblock_pb_t_kernel(
 
         def spread_small_row():
             spread = banks.tile([P, K], F32, tag="bank")
-            nc.tensor.matmul(spread[:], lhsT=ones[:], rhs=small_row[:], start=True, stop=True)
+            nc.tensor.matmul(spread[:], lhsT=ones[:, 0:P], rhs=small_row[:], start=True, stop=True)
             nc.scalar.copy(out=dt_plus[:], in_=spread[:, HALF : HALF + 1])
             nc.scalar.mul(dt_minus[:], spread[:, HALF : HALF + 1], -1.0)
             nc.scalar.copy(out=bias[:], in_=spread[:, 0:HALF].unsqueeze(1).to_broadcast([P, PAIR, HALF]))
@@ -161,6 +161,11 @@ def tile_timecrystalblock_pb_t_kernel(
                 scales=wout_scales[:],
                 in_=wout_grouped[:].rearrange("p c t -> p (c t)"),
             )
+
+        def warm_up(count):
+            unread = banks.tile([P, K], F32, tag="bank")
+            for i in range(count):
+                nc.tensor.matmul(unread[:], lhsT=ones[:, 0:P], rhs=ones[:], start=True, stop=True)
 
         h1_squared, g1_mx, state_mx = {}, {}, {}
         q_new_chunks, p_new_chunks, output_chunks = {}, {}, {}
@@ -214,9 +219,9 @@ def tile_timecrystalblock_pb_t_kernel(
             minus_dh_dp = banks.tile([P, PAIR, HALF], F32, tag="bank")
             minus_dh_dq = banks.tile([P, PAIR, HALF], F32, tag="bank")
             for i in range(PAIR):
-                multiply(minus_dh_dp, g1_mx[n], i, w1_words[:, HALF:K], w1_scales[:, HALF:K])
-            for i in range(PAIR):
                 multiply(minus_dh_dq, g1_mx[n], i, w1_words[:, 0:HALF], w1_scales[:, 0:HALF])
+            for i in range(PAIR):
+                multiply(minus_dh_dp, g1_mx[n], i, w1_words[:, HALF:K], w1_scales[:, HALF:K])
             return minus_dh_dp, minus_dh_dq
 
         def update(n, old_chunks, new_chunks, step_length, gradient):
@@ -232,15 +237,18 @@ def tile_timecrystalblock_pb_t_kernel(
 
         def transpose_state(n, values):
             c, first = where(n)
+            both = []
             for i in range(PAIR):
                 planes = banks.tile([P, PACK, P], F32, tag="bank")
+                both.append(planes)
                 for t in range(PACK):
                     source = q_new_chunks[c] if t * P < HALF else p_new_chunks[c]
                     column = (t * P) % HALF
                     nc.tensor.transpose(
                         planes[:, t, :], source[:, first + i, column : column + P], ident_f32[:]
                     )
-                nc.scalar.copy(out=values[:, 1, i * P : (i + 1) * P, :], in_=planes[:].rearrange("p t r -> p r t"))
+            for i in reversed(range(PAIR)):
+                nc.scalar.copy(out=values[:, 1, i * P : (i + 1) * P, :], in_=both[i][:].rearrange("p t r -> p r t"))
 
         def second_product(n, vector_is_free):
             c, first = where(n)
@@ -269,15 +277,16 @@ def tile_timecrystalblock_pb_t_kernel(
         def tiles_of_chunk(c):
             return slice(c * CHUNK, (c + 1) * CHUNK)
 
+        warm_up(4)
         for step in range(PAIRS + 1 + 3 * LAG):
             pair_a, pair_b = step, step - 1
             pair_c, pair_d, pair_e = pair_b - LAG, pair_b - 2 * LAG, pair_b - 3 * LAG
-            if pair_c == 0:
-                quantise_w1()
             if in_range(pair_b) or in_range(pair_d):
                 values = work.tile([P, 2, COLS, PACK], BF16, align_bytes=64)
             if in_range(pair_b):
                 form_g1(pair_b, values)
+            if pair_c == 0:
+                quantise_w1()
             if in_range(pair_a):
                 square_h1(pair_a)
             if pair_c == -1:
@@ -302,6 +311,8 @@ def tile_timecrystalblock_pb_t_kernel(
                     nc.sync.dma_start(out=p_new_rows[:, tiles_of_chunk(c), :], in_=p_new_chunks[c][:])
             if in_range(pair_b) or in_range(pair_d):
                 g1_mx[pair_b], state_mx[pair_d] = quantise(values, in_range(pair_b), in_range(pair_d))
+            if pair_c < 0:
+                warm_up(2)
             if pair_e == -1:
                 quantise_wout()
             if in_range(pair_e):

from contextlib import ExitStack

import concourse.mybir as mybir
from concourse.masks import make_identity

BF16 = mybir.dt.bfloat16
F32 = mybir.dt.float32
U32 = mybir.dt.uint32
U8 = mybir.dt.uint8
FP8X4 = mybir.dt.float8_e4m3fn_x4
ALU = mybir.AluOpType
ACT = mybir.ActivationFunctionType

P = 128
PACK = 4
BATCH = 4096
HALF = 256
K = 512
TILES = BATCH // P
PAIR = 2
PAIRS = TILES // PAIR
COLS = PAIR * P
CHUNK = 4
CHUNKS = TILES // CHUNK
PSUM_BANKS = 8
LAG = 2
ADD_PIECE = 128

FLOPS = 2 * BATCH * K * K + 2 * BATCH * K * HALF


def tile_timecrystalblock_pb_t_kernel(
    tc, h1, u, W1_qp, q, p, dt, W_out, b_out, out_0, out_1, out_2
):
    nc = tc.nc

    h1_rows = h1.rearrange("(p s) k -> p s k", s=TILES)
    u_rows = u.rearrange("(p s) k -> p s k", s=TILES)
    q_rows = q.rearrange("(p s) c -> p s c", s=TILES)
    p_rows = p.rearrange("(p s) c -> p s c", s=TILES)
    output_rows = out_0.rearrange("(p s) c -> p s c", s=TILES)
    q_new_rows = out_1.rearrange("(p s) c -> p s c", s=TILES)
    p_new_rows = out_2.rearrange("(p s) c -> p s c", s=TILES)

    with ExitStack() as ctx:
        const = ctx.enter_context(tc.tile_pool(name="const", bufs=1))
        inputs = ctx.enter_context(tc.tile_pool(name="inputs", bufs=CHUNKS))
        results = ctx.enter_context(tc.tile_pool(name="results", bufs=4))
        work = ctx.enter_context(tc.tile_pool(name="work", bufs=2))
        banks = ctx.enter_context(tc.psum_pool(name="banks", bufs=PSUM_BANKS))
        ctx.enter_context(tc.manual_schedule())

        ident_bf16 = const.tile([P, P], BF16)
        make_identity(nc, ident_bf16[:])
        ones = const.tile([P, K], BF16)
        nc.vector.memset(ones[:], 1.0)
        ident_f32 = const.tile([P, P], F32)
        make_identity(nc, ident_f32[:])
        small_row = const.tile([P, K], BF16)
        nc.gpsimd.memset(small_row[:], 0.0)

        h1_chunks, u_chunks, q_chunks, p_chunks = [], [], [], []
        for c in range(CHUNKS):
            h1_sb = inputs.tile([P, CHUNK, K], BF16)
            u_sb = inputs.tile([P, CHUNK, K], BF16)
            q_sb = inputs.tile([P, CHUNK, HALF], BF16)
            p_sb = inputs.tile([P, CHUNK, HALF], BF16)
            h1_chunks.append(h1_sb)
            u_chunks.append(u_sb)
            q_chunks.append(q_sb)
            p_chunks.append(p_sb)

        def load(rows, chunks, c, first, count):
            tile_0 = c * CHUNK + first
            nc.sync.dma_start(
                out=chunks[c][:, first : first + count, :], in_=rows[:, tile_0 : tile_0 + count, :]
            )

        wout_sb = const.tile([P, PACK, HALF], BF16)
        w1_sb = const.tile([P, PACK, K], BF16)
        load(h1_rows, h1_chunks, 0, 0, PAIR)
        load(u_rows, u_chunks, 0, 0, PAIR)
        load(h1_rows, h1_chunks, 0, PAIR, PAIR)
        load(u_rows, u_chunks, 0, PAIR, PAIR)
        load(h1_rows, h1_chunks, 1, 0, PAIR)
        nc.sync.dma_start(out=w1_sb[:], in_=W1_qp.rearrange("(a p) k -> p a k", p=P))
        nc.sync.dma_start(out=small_row[0:1, 0:HALF], in_=b_out.unsqueeze(0))
        nc.sync.dma_start(out=small_row[0:1, HALF : HALF + 1], in_=dt.unsqueeze(0))
        load(h1_rows, h1_chunks, 1, PAIR, PAIR)
        load(u_rows, u_chunks, 1, 0, PAIR)
        load(q_rows, q_chunks, 0, 0, CHUNK)
        load(p_rows, p_chunks, 0, 0, CHUNK)
        load(u_rows, u_chunks, 1, PAIR, PAIR)
        nc.sync.dma_start(out=wout_sb[:], in_=W_out.rearrange("(t p) c -> p t c", p=P))
        load(h1_rows, h1_chunks, 2, 0, CHUNK)
        load(u_rows, u_chunks, 2, 0, CHUNK)
        load(q_rows, q_chunks, 1, 0, CHUNK)
        load(p_rows, p_chunks, 1, 0, CHUNK)
        load(q_rows, q_chunks, 2, 0, CHUNK)
        load(p_rows, p_chunks, 2, 0, CHUNK)
        for c in range(3, CHUNKS):
            load(h1_rows, h1_chunks, c, 0, CHUNK)
            load(u_rows, u_chunks, c, 0, CHUNK)
            load(q_rows, q_chunks, c, 0, CHUNK)
            load(p_rows, p_chunks, c, 0, CHUNK)

        def transpose_pair(rows_sb, first):
            planes = banks.tile([P, PACK, COLS], BF16, tag="bank")
            for i in range(PAIR):
                for t in range(PACK):
                    nc.tensor.transpose(
                        planes[:, t, i * P : (i + 1) * P],
                        rows_sb[:, first + i, t * P : (t + 1) * P],
                        ident_bf16[:],
                    )
            return planes

        wout_grouped = const.tile([P, HALF, PACK], BF16, align_bytes=64)
        wout_words = const.tile([P, HALF], U32, align_bytes=64)
        wout_scales = const.tile([P, HALF], U8, align_bytes=64)
        w1_grouped = const.tile([P, K, PACK], BF16, align_bytes=64)
        w1_words = const.tile([P, K], U32, align_bytes=64)
        w1_scales = const.tile([P, K], U8, align_bytes=64)
        bias = const.tile([P, PAIR, HALF], F32)
        dt_plus = const.tile([P, 1], F32)
        dt_minus = const.tile([P, 1], F32)

        def transpose_w1():
            w1_low = transpose_pair(w1_sb, 0)
            w1_high = transpose_pair(w1_sb, PAIR)
            nc.scalar.copy(out=w1_grouped[:, 0:COLS, :], in_=w1_low[:].rearrange("p t c -> p c t"))
            nc.scalar.copy(out=w1_grouped[:, COLS:K, :], in_=w1_high[:].rearrange("p t c -> p c t"))

        def quantise_w1():
            nc.vector.quantize_mx(
                out=w1_words[:].bitcast(FP8X4),
                scales=w1_scales[:],
                in_=w1_grouped[:].rearrange("p c t -> p (c t)"),
            )

        def spread_small_row():
            spread = banks.tile([P, K], F32, tag="bank")
            nc.tensor.matmul(spread[:], lhsT=ones[:, 0:P], rhs=small_row[:], start=True, stop=True)
            nc.scalar.copy(out=dt_plus[:], in_=spread[:, HALF : HALF + 1])
            nc.scalar.mul(dt_minus[:], spread[:, HALF : HALF + 1], -1.0)
            nc.scalar.copy(out=bias[:], in_=spread[:, 0:HALF].unsqueeze(1).to_broadcast([P, PAIR, HALF]))

        def group_wout():
            nc.gpsimd.tensor_scalar(
                out=wout_grouped[:],
                in0=wout_sb[:].rearrange("p t c -> p c t"),
                scalar1=1.0,
                scalar2=0.0,
                op0=ALU.mult,
                op1=ALU.add,
            )

        def quantise_wout():
            nc.vector.quantize_mx(
                out=wout_words[:].bitcast(FP8X4),
                scales=wout_scales[:],
                in_=wout_grouped[:].rearrange("p c t -> p (c t)"),
            )

        def warm_up(count):
            unread = banks.tile([P, K], F32, tag="bank")
            for i in range(count):
                nc.tensor.matmul(unread[:], lhsT=ones[:, 0:P], rhs=ones[:], start=True, stop=True)

        h1_squared, g1_mx, state_mx = {}, {}, {}
        q_new_chunks, p_new_chunks, output_chunks = {}, {}, {}

        def where(n):
            return (n * PAIR) // CHUNK, (n * PAIR) % CHUNK

        def quantise(values, has_g1, has_state):
            words = work.tile([P, 2, COLS], U32, align_bytes=64, tag="words", bufs=LAG + 2)
            scales = work.tile([P, 2, COLS], U8, align_bytes=64, tag="scales", bufs=LAG + 2)
            halves = slice(0 if has_g1 else 1, 2 if has_state else 1)
            nc.vector.quantize_mx(
                out=words[:, halves, :].rearrange("p h c -> p (h c)").bitcast(FP8X4),
                scales=scales[:, halves, :].rearrange("p h c -> p (h c)"),
                in_=values[:, halves, :, :].rearrange("p h c t -> p (h c t)"),
            )
            return [(words[:, h, :], scales[:, h, :]) for h in range(2)]

        def multiply(product, stationary, i, moving_words, moving_scales):
            words, scales = stationary
            nc.tensor.matmul_mx(
                out=product[:, i, :],
                lhsT=words[:, i * P : (i + 1) * P].bitcast(FP8X4),
                lhsT_scale=scales[:, i * P : (i + 1) * P],
                rhs=moving_words.bitcast(FP8X4),
                rhs_scale=moving_scales,
                start=True,
                stop=True,
            )

        def square_h1(n):
            c, first = where(n)
            h1_planes = transpose_pair(h1_chunks[c], first)
            squared = work.tile([P, COLS, PACK], F32, tag="h1_squared", bufs=3)
            nc.scalar.activation(out=squared[:], in_=h1_planes[:].rearrange("p t c -> p c t"), func=ACT.Square)
            h1_squared[n] = squared

        def form_g1(n, values):
            c, first = where(n)
            u_planes = transpose_pair(u_chunks[c], first)
            nc.vector.scalar_tensor_tensor(
                out=values[:, 0, :, :],
                in0=h1_squared[n][:],
                scalar=1.0,
                in1=u_planes[:].rearrange("p t c -> p c t"),
                op0=ALU.subtract,
                op1=ALU.mult,
            )

        def first_product(n):
            minus_dh_dp = banks.tile([P, PAIR, HALF], F32, tag="bank")
            minus_dh_dq = banks.tile([P, PAIR, HALF], F32, tag="bank")
            for i in range(PAIR):
                multiply(minus_dh_dq, g1_mx[n], i, w1_words[:, 0:HALF], w1_scales[:, 0:HALF])
            for i in range(PAIR):
                multiply(minus_dh_dp, g1_mx[n], i, w1_words[:, HALF:K], w1_scales[:, HALF:K])
            return minus_dh_dp, minus_dh_dq

        def update(n, old_chunks, new_chunks, step_length, gradient):
            c, first = where(n)
            nc.vector.scalar_tensor_tensor(
                out=new_chunks[c][:, first : first + PAIR, :],
                in0=gradient[:],
                scalar=step_length[:, 0:1],
                in1=old_chunks[c][:, first : first + PAIR, :],
                op0=ALU.mult,
                op1=ALU.add,
            )

        def transpose_state(n, values):
            c, first = where(n)
            both = []
            for i in range(PAIR):
                planes = banks.tile([P, PACK, P], F32, tag="bank")
                both.append(planes)
                for t in range(PACK):
                    source = q_new_chunks[c] if t * P < HALF else p_new_chunks[c]
                    column = (t * P) % HALF
                    nc.tensor.transpose(
                        planes[:, t, :], source[:, first + i, column : column + P], ident_f32[:]
                    )
            for i in reversed(range(PAIR)):
                nc.scalar.copy(out=values[:, 1, i * P : (i + 1) * P, :], in_=both[i][:].rearrange("p t r -> p r t"))

        def second_product(n, vector_is_free):
            c, first = where(n)
            product = banks.tile([P, PAIR, HALF], F32, tag="bank")
            for i in range(PAIR):
                multiply(product, state_mx[n], i, wout_words[:], wout_scales[:])
            output_pair = output_chunks[c][:, first : first + PAIR, :]
            if vector_is_free:
                nc.vector.tensor_tensor(out=output_pair, in0=product[:], in1=bias[:], op=ALU.add)
            else:
                unbiased = work.tile([P, PAIR, HALF], F32)
                nc.scalar.copy(out=unbiased[:], in_=product[:])
                for i in range(PAIR):
                    for start in range(0, HALF, ADD_PIECE):
                        piece = slice(start, start + ADD_PIECE)
                        nc.gpsimd.tensor_tensor(
                            out=output_pair[:, i, piece], in0=unbiased[:, i, piece], in1=bias[:, i, piece], op=ALU.add
                        )

        def last_of_chunk(n):
            return (n + 1) * PAIR % CHUNK == 0

        def in_range(n):
            return 0 <= n < PAIRS

        def tiles_of_chunk(c):
            return slice(c * CHUNK, (c + 1) * CHUNK)

        warm_up(4)
        for step in range(PAIRS + 1 + 3 * LAG):
            pair_a, pair_b = step, step - 1
            pair_c, pair_d, pair_e = pair_b - LAG, pair_b - 2 * LAG, pair_b - 3 * LAG
            if in_range(pair_b) or in_range(pair_d):
                values = work.tile([P, 2, COLS, PACK], BF16, align_bytes=64)
            if in_range(pair_b):
                form_g1(pair_b, values)
            if pair_c == 0:
                quantise_w1()
            if in_range(pair_a):
                square_h1(pair_a)
            if pair_c == -1:
                transpose_w1()
                spread_small_row()
            if pair_d == -1:
                group_wout()
            if in_range(pair_d):
                transpose_state(pair_d, values)
            if in_range(pair_c):
                c, first = where(pair_c)
                if first == 0:
                    q_new_sb = results.tile([P, CHUNK, HALF], F32)
                    p_new_sb = results.tile([P, CHUNK, HALF], F32)
                    q_new_chunks[c] = q_new_sb
                    p_new_chunks[c] = p_new_sb
                minus_dh_dp, minus_dh_dq = first_product(pair_c)
                update(pair_c, q_chunks, q_new_chunks, dt_minus, minus_dh_dp)
                update(pair_c, p_chunks, p_new_chunks, dt_plus, minus_dh_dq)
                if last_of_chunk(pair_c):
                    nc.sync.dma_start(out=q_new_rows[:, tiles_of_chunk(c), :], in_=q_new_chunks[c][:])
                    nc.sync.dma_start(out=p_new_rows[:, tiles_of_chunk(c), :], in_=p_new_chunks[c][:])
            if in_range(pair_b) or in_range(pair_d):
                g1_mx[pair_b], state_mx[pair_d] = quantise(values, in_range(pair_b), in_range(pair_d))
            if pair_c < 0:
                warm_up(2)
            if pair_e == -1:
                quantise_wout()
            if in_range(pair_e):
                c, first = where(pair_e)
                if first == 0:
                    output_sb = results.tile([P, CHUNK, HALF], F32)
                    output_chunks[c] = output_sb
                second_product(pair_e, vector_is_free=pair_c >= PAIRS)
                if last_of_chunk(pair_e):
                    nc.sync.dma_start(out=output_rows[:, tiles_of_chunk(c), :], in_=output_chunks[c][:])
